import numpy as np
import ml_dtypes


def mxq(x, axis, fmt="e4m3"):
    dtype, down = {"e4m3": (ml_dtypes.float8_e4m3fn, 7), "e5m2": (ml_dtypes.float8_e5m2, 14)}[fmt]
    v = np.moveaxis(np.asarray(x, np.float32).astype(ml_dtypes.bfloat16).astype(np.float64), axis, -1)
    blocks = v.reshape(v.shape[:-1] + (-1, 32))
    amax = np.abs(blocks).max(-1, keepdims=True)
    byte = np.maximum(np.where(amax > 0, np.frexp(amax)[1] - 1 + 127, 0) - down, 1)
    scale = np.exp2(byte - 127.0)
    codes = (blocks / scale).astype(np.float32).astype(dtype).astype(np.float64)
    return np.moveaxis((codes * scale).reshape(v.shape), -1, axis)


WIDE = False


def mx_kscale(k):
    if not WIDE:
        return np.ones(k)
    levels = np.array([10, -10, 5, -5, 0])
    if k % 512:
        return np.exp2(np.random.permutation(np.resize(levels, k // 32))).repeat(32)
    a = np.empty((k // 512, 16))
    for p in range(k // 512):
        a[p, :8] = np.random.permutation(np.resize(levels, 8))
        for g in range(8):
            far = levels[np.abs(levels - a[p, g]) >= 10]
            a[p, g + 8] = far[np.random.randint(len(far))]
    return np.exp2(a.ravel()).repeat(32)


BF16 = ml_dtypes.bfloat16


def bf(x):
    return np.asarray(x, np.float32).astype(BF16)


def f64(x):
    return np.asarray(x).astype(np.float64)


ND, NS, D0, D1, D2, D3, DH, C = 2048, 2048, 512, 128, 256, 512, 256, 10
SIG = 4.0


def draw_adj():
    w = np.exp(SIG * np.random.standard_normal((ND, NS)))
    return w / w.sum(1, keepdims=True)


def setup_inputs():
    u = mx_kscale(NS)
    return {"x1": bf(np.maximum(np.random.standard_normal((NS, D1)), 0.0) / u[:, None]),
            "adj": bf(draw_adj() * u),
            "W1": bf(np.random.standard_normal((D1, D2)) * 2.0 / np.sqrt(D1)),
            "b1": bf(np.random.standard_normal(D2) * 0.5 / u.max())}


def reference(x1, adj, W1, b1):
    h = f64(x1) @ f64(W1) + f64(b1)
    return np.maximum(mxq(f64(adj), 1, "e4m3") @ mxq(h, 0, "e4m3"), 0.0)

@@ -1,0 +1,173 @@
+from contextlib import ExitStack
+
+import concourse.mybir as mybir
+from concourse.masks import make_identity
+
+F32 = mybir.dt.float32
+BF16 = mybir.dt.bfloat16
+U32 = mybir.dt.uint32
+U8 = mybir.dt.uint8
+FP8X4 = mybir.dt.float8_e4m3fn_x4
+
+P = 128
+PACK = 4
+K_PASS = P * PACK
+BANK = 512
+
+N_DST, N_SRC, D_IN, D_OUT = 2048, 2048, 128, 256
+PASSES = N_SRC // K_PASS
+DST_TILES = N_DST // P
+SLOTS = PASSES * PACK
+WORDS = N_SRC // 2
+ROUND = 2
+ROUNDS = DST_TILES // ROUND
+BUNCH = 2
+assert PASSES == BUNCH * ROUND
+
+FLOPS = 2 * N_DST * N_SRC * D_OUT + 2 * N_SRC * D_IN * D_OUT
+
+
+def tile_gcn_pb_kernel(tc, x1, adj, W1, b1, out):
+    nc = tc.nc
+    with ExitStack() as ctx:
+        ctx.enter_context(tc.manual_schedule())
+        keep = ctx.enter_context(tc.tile_pool(name="keep", bufs=1))
+        stage = ctx.enter_context(tc.tile_pool(name="stage", bufs=2 * BUNCH * ROUND))
+        psum_t = ctx.enter_context(tc.psum_pool(name="psum_t", bufs=6))
+        psum_mm = ctx.enter_context(tc.psum_pool(name="psum_mm", bufs=2))
+
+        bias_rows = keep.tile([P, D_OUT], BF16, name="bias_rows")
+        nc.vector.memset(bias_rows[:], 0.0)
+        nc.sync.dma_start(out=bias_rows[0:1, :], in_=b1.rearrange("(o f) -> o f", o=1))
+        w1_sb = keep.tile([P, D_OUT], BF16, name="w1_sb")
+        nc.sync.dma_start(out=w1_sb[:], in_=W1)
+        x1_sb = keep.tile([P, SLOTS * D_IN], BF16, name="x1_sb")
+        nc.sync.dma_start(
+            out=x1_sb[:].rearrange("p (g w) -> p g w", w=PACK * D_IN),
+            in_=x1.rearrange("(g p t) d -> p g (t d)", p=P, t=PACK),
+        )
+        adj_rows = adj.rearrange("(p a) k -> p (a k)", a=DST_TILES)
+        adj_sb = []
+        for r in range(ROUNDS):
+            adj_r = keep.tile([P, ROUND * N_SRC], BF16, name="adj%d" % r)
+            nc.sync.dma_start(
+                out=adj_r[:], in_=adj_rows[:, r * ROUND * N_SRC : (r + 1) * ROUND * N_SRC]
+            )
+            adj_sb.append(adj_r)
+
+        ident_bf = keep.tile([P, P], BF16, name="ident_bf")
+        make_identity(nc, ident_bf[:])
+        ident_f32 = keep.tile([P, P], F32, name="ident_f32")
+        make_identity(nc, ident_f32[:])
+        ones = keep.tile([P, P], BF16, name="ones")
+        nc.vector.memset(ones[:], 1.0)
+
+        bias_ps = psum_mm.tile([P, D_OUT], F32, tag="mm")
+        nc.tensor.matmul(out=bias_ps[:], lhsT=ones[:], rhs=bias_rows[:], start=True, stop=True)
+        bias_all = keep.tile([P, D_OUT], F32, name="bias_all")
+        nc.vector.tensor_copy(out=bias_all[:], in_=bias_ps[:])
+
+        x1T = keep.tile([P, SLOTS * P], BF16, name="x1T")
+        for j in range(SLOTS // PACK):
+            x1T_ps = psum_t.tile([P, PACK * P], BF16, tag="t")
+            for t in range(PACK):
+                s = PACK * j + t
+                nc.tensor.transpose(
+                    x1T_ps[:, t * P : (t + 1) * P], x1_sb[:, s * D_IN : (s + 1) * D_IN], ident_bf[:]
+                )
+            nc.scalar.copy(out=x1T[:, j * PACK * P : (j + 1) * PACK * P], in_=x1T_ps[:])
+
+        h_grouped = keep.tile([P, PASSES * D_OUT * PACK], BF16, name="h_grouped", align_bytes=64)
+        h_grouped_v = h_grouped[:].rearrange("p (g f t) -> p g f t", g=PASSES, t=PACK)
+
+        def h_pass(g):
+            for f0 in range(0, D_OUT, P):
+                h_ps = psum_mm.tile([P, BANK], F32, tag="mm")
+                for t in range(PACK):
+                    s = PACK * g + t
+                    nc.tensor.matmul(
+                        out=h_ps[:, t * P : (t + 1) * P],
+                        lhsT=x1T[:, s * P : (s + 1) * P],
+                        rhs=w1_sb[:, f0 : f0 + P],
+                        start=True,
+                        stop=True,
+                    )
+                nc.vector.tensor_tensor(
+                    out=h_grouped_v[:, g, f0 : f0 + P, :],
+                    in0=h_ps[:].rearrange("p (t f) -> p f t", t=PACK),
+                    in1=bias_all[:, f0 : f0 + P].unsqueeze(2).to_broadcast([P, P, PACK]),
+                    op=mybir.AluOpType.add,
+                )
+
+        grouped = {}
+        codes = {}
+
+        def transpose_tile(a):
+            adj_words = adj_sb[a // ROUND][:].bitcast(F32)
+            first = (a % ROUND) * WORDS
+            grouped[a] = stage.tile([P, N_SRC], BF16, name="grouped", align_bytes=64)
+            grouped_words = grouped[a][:].bitcast(F32)
+            for b in range(WORDS // BANK):
+                adjT_ps = psum_t.tile([P, BANK], F32, tag="t")
+                for j in range(BANK // P):
+                    w0 = first + b * BANK + (j // 2) * 2 * P + j % 2
+                    nc.tensor.transpose(
+                        adjT_ps[:, j * P : (j + 1) * P],
+                        adj_words[:, w0 : w0 + 2 * P - 1 : 2],
+                        ident_f32[:],
+                    )
+                nc.scalar.copy(
+                    out=grouped_words[:, b * BANK : (b + 1) * BANK].rearrange(
+                        "p (g i u) -> p g i u", i=P, u=2
+                    ),
+                    in_=adjT_ps[:].rearrange("p (g u i) -> p g i u", i=P, u=2),
+                )
+
+        def quantise_tile(a):
+            packed = stage.tile([P, PASSES * P], U32, name="adj_packed", align_bytes=64)
+            scales = stage.tile([P, PASSES * P], U8, name="adj_scales", align_bytes=64)
+            nc.vector.quantize_mx(out=packed[:].bitcast(FP8X4), scales=scales[:], in_=grouped[a][:])
+            codes[a] = (packed, scales)
+
+        def multiply_tile(a, acc):
+            packed, scales = codes[a]
+            for g in range(PASSES):
+                nc.tensor.matmul_mx(
+                    out=acc,
+                    lhsT=packed[:, g * P : (g + 1) * P].bitcast(FP8X4),
+                    lhsT_scale=scales[:, g * P : (g + 1) * P],
+                    rhs=h_packed[:, g * D_OUT : (g + 1) * D_OUT].bitcast(FP8X4),
+                    rhs_scale=h_scales[:, g * D_OUT : (g + 1) * D_OUT],
+                    start=(g == 0),
+                    stop=(g == PASSES - 1),
+                )
+
+        def tiles_of(r):
+            return range(r * ROUND, (r + 1) * ROUND)
+
+        for g in range(PASSES):
+            h_pass(g)
+            transpose_tile(g)
+        h_packed = keep.tile([P, PASSES * D_OUT], U32, name="h_packed", align_bytes=64)
+        h_scales = keep.tile([P, PASSES * D_OUT], U8, name="h_scales", align_bytes=64)
+        nc.vector.quantize_mx(out=h_packed[:].bitcast(FP8X4), scales=h_scales[:], in_=h_grouped[:])
+        for r in range(BUNCH):
+            for a in tiles_of(r):
+                quantise_tile(a)
+
+        out_sb = keep.tile([P, DST_TILES * D_OUT], F32, name="out_sb")
+        out_rows = out.rearrange("(p a) f -> p (a f)", a=DST_TILES)
+        for first in range(0, ROUNDS, BUNCH):
+            for r in range(first + BUNCH, min(first + 2 * BUNCH, ROUNDS)):
+                for a in tiles_of(r):
+                    transpose_tile(a)
+            for r in range(first, first + BUNCH):
+                if r + BUNCH < ROUNDS:
+                    for a in tiles_of(r + BUNCH):
+                        quantise_tile(a)
+                acc = psum_mm.tile([P, BANK], F32, tag="mm")
+                for a in tiles_of(r):
+                    multiply_tile(a, acc[:, (a % ROUND) * D_OUT : (a % ROUND + 1) * D_OUT])
+                cols = slice(r * BANK, (r + 1) * BANK)
+                nc.vector.tensor_scalar_max(out=out_sb[:, cols], in0=acc[:], scalar1=0.0)
+                nc.sync.dma_start(out=out_rows[:, cols], in_=out_sb[:, cols])

@@ -21,8 +21,8 @@ SLOTS = PASSES * PACK
 WORDS = N_SRC // 2
 ROUND = 2
 ROUNDS = DST_TILES // ROUND
-BUNCH = 2
-assert PASSES == BUNCH * ROUND
+LEAD = 5
+STEPPED = LEAD
 
 FLOPS = 2 * N_DST * N_SRC * D_OUT + 2 * N_SRC * D_IN * D_OUT
 
@@ -32,28 +32,28 @@ def tile_gcn_pb_kernel(tc, x1, adj, W1, b1, out):
     with ExitStack() as ctx:
         ctx.enter_context(tc.manual_schedule())
         keep = ctx.enter_context(tc.tile_pool(name="keep", bufs=1))
-        stage = ctx.enter_context(tc.tile_pool(name="stage", bufs=2 * BUNCH * ROUND))
+        stage = ctx.enter_context(tc.tile_pool(name="stage", bufs=8))
         psum_t = ctx.enter_context(tc.psum_pool(name="psum_t", bufs=6))
         psum_mm = ctx.enter_context(tc.psum_pool(name="psum_mm", bufs=2))
 
+        x1_sb = keep.tile([P, SLOTS * D_IN], BF16, name="x1_sb")
+        x1_rows = x1.rearrange("(g p t) d -> g p (t d)", p=P, t=PACK)
         bias_rows = keep.tile([P, D_OUT], BF16, name="bias_rows")
         nc.vector.memset(bias_rows[:], 0.0)
-        nc.sync.dma_start(out=bias_rows[0:1, :], in_=b1.rearrange("(o f) -> o f", o=1))
         w1_sb = keep.tile([P, D_OUT], BF16, name="w1_sb")
+        nc.sync.dma_start(out=x1_sb[:, 0 : PACK * D_IN], in_=x1_rows[0])
         nc.sync.dma_start(out=w1_sb[:], in_=W1)
-        x1_sb = keep.tile([P, SLOTS * D_IN], BF16, name="x1_sb")
-        nc.sync.dma_start(
-            out=x1_sb[:].rearrange("p (g w) -> p g w", w=PACK * D_IN),
-            in_=x1.rearrange("(g p t) d -> p g (t d)", p=P, t=PACK),
-        )
-        adj_rows = adj.rearrange("(p a) k -> p (a k)", a=DST_TILES)
-        adj_sb = []
-        for r in range(ROUNDS):
-            adj_r = keep.tile([P, ROUND * N_SRC], BF16, name="adj%d" % r)
+        nc.sync.dma_start(out=bias_rows[0:1, :], in_=b1.rearrange("(o f) -> o f", o=1))
+        for g in range(1, PASSES):
             nc.sync.dma_start(
-                out=adj_r[:], in_=adj_rows[:, r * ROUND * N_SRC : (r + 1) * ROUND * N_SRC]
+                out=x1_sb[:, g * PACK * D_IN : (g + 1) * PACK * D_IN], in_=x1_rows[g]
             )
-            adj_sb.append(adj_r)
+        adj_rows = adj.rearrange("(p a) k -> p a k", a=DST_TILES)
+        adj_sb = []
+        for a in range(DST_TILES):
+            adj_a = keep.tile([P, N_SRC], BF16, name="adj%d" % a)
+            nc.sync.dma_start(out=adj_a[:], in_=adj_rows[:, a, :])
+            adj_sb.append(adj_a)
 
         ident_bf = keep.tile([P, P], BF16, name="ident_bf")
         make_identity(nc, ident_bf[:])
@@ -61,67 +61,91 @@ def tile_gcn_pb_kernel(tc, x1, adj, W1, b1, out):
         make_identity(nc, ident_f32[:])
         ones = keep.tile([P, P], BF16, name="ones")
         nc.vector.memset(ones[:], 1.0)
-
-        bias_ps = psum_mm.tile([P, D_OUT], F32, tag="mm")
-        nc.tensor.matmul(out=bias_ps[:], lhsT=ones[:], rhs=bias_rows[:], start=True, stop=True)
         bias_all = keep.tile([P, D_OUT], F32, name="bias_all")
-        nc.vector.tensor_copy(out=bias_all[:], in_=bias_ps[:])
-
         x1T = keep.tile([P, SLOTS * P], BF16, name="x1T")
-        for j in range(SLOTS // PACK):
+        h_grouped = keep.tile([P, PASSES * D_OUT * PACK], BF16, name="h_grouped", align_bytes=64)
+        h_grouped_v = h_grouped[:].rearrange("p (g f t) -> p g f t", g=PASSES, t=PACK)
+        h_packed = keep.tile([P, PASSES * D_OUT], U32, name="h_packed", align_bytes=64)
+        h_scales = keep.tile([P, PASSES * D_OUT], U8, name="h_scales", align_bytes=64)
+
+        def spread_bias():
+            bias_ps = psum_mm.tile([P, D_OUT], F32, tag="mm")
+            nc.tensor.matmul(out=bias_ps[:], lhsT=ones[:], rhs=bias_rows[:], start=True, stop=True)
+            nc.vector.tensor_copy(out=bias_all[:], in_=bias_ps[:])
+
+        def transpose_x1(g):
             x1T_ps = psum_t.tile([P, PACK * P], BF16, tag="t")
             for t in range(PACK):
-                s = PACK * j + t
+                s = PACK * g + t
                 nc.tensor.transpose(
                     x1T_ps[:, t * P : (t + 1) * P], x1_sb[:, s * D_IN : (s + 1) * D_IN], ident_bf[:]
                 )
-            nc.scalar.copy(out=x1T[:, j * PACK * P : (j + 1) * PACK * P], in_=x1T_ps[:])
+            nc.scalar.copy(out=x1T[:, g * PACK * P : (g + 1) * PACK * P], in_=x1T_ps[:])
 
-        h_grouped = keep.tile([P, PASSES * D_OUT * PACK], BF16, name="h_grouped", align_bytes=64)
-        h_grouped_v = h_grouped[:].rearrange("p (g f t) -> p g f t", g=PASSES, t=PACK)
-
-        def h_pass(g):
-            for f0 in range(0, D_OUT, P):
-                h_ps = psum_mm.tile([P, BANK], F32, tag="mm")
-                for t in range(PACK):
-                    s = PACK * g + t
-                    nc.tensor.matmul(
-                        out=h_ps[:, t * P : (t + 1) * P],
-                        lhsT=x1T[:, s * P : (s + 1) * P],
-                        rhs=w1_sb[:, f0 : f0 + P],
-                        start=True,
-                        stop=True,
-                    )
-                nc.vector.tensor_tensor(
-                    out=h_grouped_v[:, g, f0 : f0 + P, :],
-                    in0=h_ps[:].rearrange("p (t f) -> p f t", t=PACK),
-                    in1=bias_all[:, f0 : f0 + P].unsqueeze(2).to_broadcast([P, P, PACK]),
-                    op=mybir.AluOpType.add,
+        def h_half(g, f0):
+            h_ps = psum_mm.tile([P, BANK], F32, tag="mm")
+            for t in range(PACK):
+                s = PACK * g + t
+                nc.tensor.matmul(
+                    out=h_ps[:, t * P : (t + 1) * P],
+                    lhsT=x1T[:, s * P : (s + 1) * P],
+                    rhs=w1_sb[:, f0 : f0 + P],
+                    start=True,
+                    stop=True,
                 )
+            nc.vector.tensor_tensor(
+                out=h_grouped_v[:, g, f0 : f0 + P, :],
+                in0=h_ps[:].rearrange("p (t f) -> p f t", t=PACK),
+                in1=bias_all[:, f0 : f0 + P].unsqueeze(2).to_broadcast([P, P, PACK]),
+                op=mybir.AluOpType.add,
+            )
 
+        def quantise_h(g):
+            words = slice(g * D_OUT, (g + 1) * D_OUT)
+            nc.vector.quantize_mx(
+                out=h_packed[:, words].bitcast(FP8X4),
+                scales=h_scales[:, words],
+                in_=h_grouped[:, g * D_OUT * PACK : (g + 1) * D_OUT * PACK],
+            )
+
+        even_odd = {}
         grouped = {}
         codes = {}
 
-        def transpose_tile(a):
-            adj_words = adj_sb[a // ROUND][:].bitcast(F32)
-            first = (a % ROUND) * WORDS
-            grouped[a] = stage.tile([P, N_SRC], BF16, name="grouped", align_bytes=64)
-            grouped_words = grouped[a][:].bitcast(F32)
-            for b in range(WORDS // BANK):
-                adjT_ps = psum_t.tile([P, BANK], F32, tag="t")
-                for j in range(BANK // P):
-                    w0 = first + b * BANK + (j // 2) * 2 * P + j % 2
-                    nc.tensor.transpose(
-                        adjT_ps[:, j * P : (j + 1) * P],
-                        adj_words[:, w0 : w0 + 2 * P - 1 : 2],
-                        ident_f32[:],
-                    )
-                nc.scalar.copy(
-                    out=grouped_words[:, b * BANK : (b + 1) * BANK].rearrange(
-                        "p (g i u) -> p g i u", i=P, u=2
-                    ),
-                    in_=adjT_ps[:].rearrange("p (g u i) -> p g i u", i=P, u=2),
+        def words_of(a):
+            return adj_sb[a][:].bitcast(F32)
+
+        def sort_tile(a):
+            even_odd[a] = stage.tile([P, WORDS], F32, name="even_odd")
+            nc.vector.tensor_copy(
+                out=even_odd[a][:].rearrange("p (u w) -> p u w", u=2),
+                in_=words_of(a).rearrange("p (w u) -> p u w", u=2),
+            )
+
+        def half_pass(a, g, u):
+            if a < STEPPED:
+                return words_of(a)[:, 2 * P * g + u : 2 * P * (g + 1) - 1 + u : 2]
+            w0 = u * (WORDS // 2) + g * P
+            return even_odd[a][:, w0 : w0 + P]
+
+        def transpose_half(a, b):
+            if b == 0:
+                grouped[a] = stage.tile([P, N_SRC], BF16, name="grouped", align_bytes=64)
+            adjT_ps = psum_t.tile([P, BANK], F32, tag="t")
+            for j in range(BANK // P):
+                nc.tensor.transpose(
+                    adjT_ps[:, j * P : (j + 1) * P], half_pass(a, 2 * b + j // 2, j % 2), ident_f32[:]
                 )
+            nc.scalar.copy(
+                out=grouped[a][:].bitcast(F32)[:, b * BANK : (b + 1) * BANK].rearrange(
+                    "p (g i u) -> p g i u", i=P, u=2
+                ),
+                in_=adjT_ps[:].rearrange("p (g u i) -> p g i u", i=P, u=2),
+            )
+
+        def transpose_tile(a):
+            for b in range(WORDS // BANK):
+                transpose_half(a, b)
 
         def quantise_tile(a):
             packed = stage.tile([P, PASSES * P], U32, name="adj_packed", align_bytes=64)
@@ -143,31 +167,45 @@ def tile_gcn_pb_kernel(tc, x1, adj, W1, b1, out):
                 )
 
         def tiles_of(r):
-            return range(r * ROUND, (r + 1) * ROUND)
-
-        for g in range(PASSES):
-            h_pass(g)
-            transpose_tile(g)
-        h_packed = keep.tile([P, PASSES * D_OUT], U32, name="h_packed", align_bytes=64)
-        h_scales = keep.tile([P, PASSES * D_OUT], U8, name="h_scales", align_bytes=64)
-        nc.vector.quantize_mx(out=h_packed[:].bitcast(FP8X4), scales=h_scales[:], in_=h_grouped[:])
-        for r in range(BUNCH):
-            for a in tiles_of(r):
-                quantise_tile(a)
+            return range(r * ROUND, (r + 1) * ROUND) if r < ROUNDS else range(0)
 
         out_sb = keep.tile([P, DST_TILES * D_OUT], F32, name="out_sb")
         out_rows = out.rearrange("(p a) f -> p (a f)", a=DST_TILES)
-        for first in range(0, ROUNDS, BUNCH):
-            for r in range(first + BUNCH, min(first + 2 * BUNCH, ROUNDS)):
-                for a in tiles_of(r):
-                    transpose_tile(a)
-            for r in range(first, first + BUNCH):
-                if r + BUNCH < ROUNDS:
-                    for a in tiles_of(r + BUNCH):
-                        quantise_tile(a)
-                acc = psum_mm.tile([P, BANK], F32, tag="mm")
-                for a in tiles_of(r):
-                    multiply_tile(a, acc[:, (a % ROUND) * D_OUT : (a % ROUND + 1) * D_OUT])
-                cols = slice(r * BANK, (r + 1) * BANK)
-                nc.vector.tensor_scalar_max(out=out_sb[:, cols], in0=acc[:], scalar1=0.0)
-                nc.sync.dma_start(out=out_rows[:, cols], in_=out_sb[:, cols])
+
+        def multiply_round(r):
+            acc = psum_mm.tile([P, BANK], F32, tag="mm")
+            for a in tiles_of(r):
+                multiply_tile(a, acc[:, (a % ROUND) * D_OUT : (a % ROUND + 1) * D_OUT])
+            return acc
+
+        def store_round(r, acc):
+            cols = slice(r * BANK, (r + 1) * BANK)
+            nc.scalar.activation(
+                out=out_sb[:, cols], in_=acc[:], func=mybir.ActivationFunctionType.Relu
+            )
+            nc.sync.dma_start(out=out_rows[:, cols], in_=out_sb[:, cols])
+
+        for g in range(PASSES):
+            transpose_x1(g)
+        spread_bias()
+        halves = [(a, b) for a in range(LEAD) for b in range(WORDS // BANK)]
+        for g in range(PASSES):
+            for f0 in range(0, D_OUT, P):
+                if g > 0:
+                    transpose_half(*halves.pop(0))
+                h_half(g, f0)
+            if g > 0:
+                quantise_h(g - 1)
+        for a, b in halves:
+            transpose_half(a, b)
+        quantise_h(PASSES - 1)
+
+        for r in range(ROUNDS):
+            for a in tiles_of(r):
+                if a + LEAD < DST_TILES:
+                    sort_tile(a + LEAD)
+                quantise_tile(a)
+            for a in tiles_of(r):
+                if a + LEAD < DST_TILES:
+                    transpose_tile(a + LEAD)
+            store_round(r, multiply_round(r))

@@ -21,6 +21,7 @@ SLOTS = PASSES * PACK
 WORDS = N_SRC // 2
 ROUND = 2
 ROUNDS = DST_TILES // ROUND
+WARM_UP = 3
 LEAD = 5
 STEPPED = LEAD
 
@@ -36,10 +37,17 @@ def tile_gcn_pb_kernel(tc, x1, adj, W1, b1, out):
         psum_t = ctx.enter_context(tc.psum_pool(name="psum_t", bufs=6))
         psum_mm = ctx.enter_context(tc.psum_pool(name="psum_mm", bufs=2))
 
-        x1_sb = keep.tile([P, SLOTS * D_IN], BF16, name="x1_sb")
-        x1_rows = x1.rearrange("(g p t) d -> g p (t d)", p=P, t=PACK)
         bias_rows = keep.tile([P, D_OUT], BF16, name="bias_rows")
         nc.vector.memset(bias_rows[:], 0.0)
+
+        zeros = keep.tile([P, BANK], BF16, name="zeros")
+        nc.vector.memset(zeros[:], 0.0)
+        idle_ps = psum_mm.tile([P, BANK], F32, tag="mm")
+        for _ in range(WARM_UP):
+            nc.tensor.matmul(out=idle_ps[:], lhsT=zeros[:, 0:P], rhs=zeros[:], start=True, stop=True)
+
+        x1_sb = keep.tile([P, SLOTS * D_IN], BF16, name="x1_sb")
+        x1_rows = x1.rearrange("(g p t) d -> g p (t d)", p=P, t=PACK)
         w1_sb = keep.tile([P, D_OUT], BF16, name="w1_sb")
         nc.sync.dma_start(out=x1_sb[:, 0 : PACK * D_IN], in_=x1_rows[0])
         nc.sync.dma_start(out=w1_sb[:], in_=W1)
@@ -57,10 +65,10 @@ def tile_gcn_pb_kernel(tc, x1, adj, W1, b1, out):
 
         ident_bf = keep.tile([P, P], BF16, name="ident_bf")
         make_identity(nc, ident_bf[:])
-        ident_f32 = keep.tile([P, P], F32, name="ident_f32")
-        make_identity(nc, ident_f32[:])
         ones = keep.tile([P, P], BF16, name="ones")
         nc.vector.memset(ones[:], 1.0)
+        ident_f32 = keep.tile([P, P], F32, name="ident_f32")
+        make_identity(nc, ident_f32[:])
         bias_all = keep.tile([P, D_OUT], F32, name="bias_all")
         x1T = keep.tile([P, SLOTS * P], BF16, name="x1T")
         h_grouped = keep.tile([P, PASSES * D_OUT * PACK], BF16, name="h_grouped", align_bytes=64)
@@ -172,28 +180,34 @@ def tile_gcn_pb_kernel(tc, x1, adj, W1, b1, out):
         out_sb = keep.tile([P, DST_TILES * D_OUT], F32, name="out_sb")
         out_rows = out.rearrange("(p a) f -> p (a f)", a=DST_TILES)
 
-        def multiply_round(r):
+        def finish_round(r):
             acc = psum_mm.tile([P, BANK], F32, tag="mm")
             for a in tiles_of(r):
                 multiply_tile(a, acc[:, (a % ROUND) * D_OUT : (a % ROUND + 1) * D_OUT])
-            return acc
-
-        def store_round(r, acc):
             cols = slice(r * BANK, (r + 1) * BANK)
             nc.scalar.activation(
                 out=out_sb[:, cols], in_=acc[:], func=mybir.ActivationFunctionType.Relu
             )
             nc.sync.dma_start(out=out_rows[:, cols], in_=out_sb[:, cols])
 
-        for g in range(PASSES):
-            transpose_x1(g)
+        def finish_tile(a):
+            acc = psum_t.tile([P, D_OUT], F32, tag="t")
+            multiply_tile(a, acc[:])
+            cols = slice(a * D_OUT, (a + 1) * D_OUT)
+            nc.vector.tensor_scalar_max(out=out_sb[:, cols], in0=acc[:], scalar1=0.0)
+            nc.sync.dma_start(out=out_rows[:, cols], in_=out_sb[:, cols])
+
+        transpose_x1(0)
         spread_bias()
+        transpose_x1(1)
         halves = [(a, b) for a in range(LEAD) for b in range(WORDS // BANK)]
         for g in range(PASSES):
             for f0 in range(0, D_OUT, P):
                 if g > 0:
                     transpose_half(*halves.pop(0))
                 h_half(g, f0)
+            if g + 2 < PASSES:
+                transpose_x1(g + 2)
             if g > 0:
                 quantise_h(g - 1)
         for a, b in halves:
@@ -208,4 +222,8 @@ def tile_gcn_pb_kernel(tc, x1, adj, W1, b1, out):
             for a in tiles_of(r):
                 if a + LEAD < DST_TILES:
                     transpose_tile(a + LEAD)
-            store_round(r, multiply_round(r))
+            if r < ROUNDS - 1:
+                finish_round(r)
+            else:
+                for a in tiles_of(r):
+                    finish_tile(a)

@@ -21,7 +21,6 @@ SLOTS = PASSES * PACK
 WORDS = N_SRC // 2
 ROUND = 2
 ROUNDS = DST_TILES // ROUND
-WARM_UP = 3
 LEAD = 5
 STEPPED = LEAD
 
@@ -39,12 +38,6 @@ def tile_gcn_pb_kernel(tc, x1, adj, W1, b1, out):
 
         bias_rows = keep.tile([P, D_OUT], BF16, name="bias_rows")
         nc.vector.memset(bias_rows[:], 0.0)
-
-        zeros = keep.tile([P, BANK], BF16, name="zeros")
-        nc.vector.memset(zeros[:], 0.0)
-        idle_ps = psum_mm.tile([P, BANK], F32, tag="mm")
-        for _ in range(WARM_UP):
-            nc.tensor.matmul(out=idle_ps[:], lhsT=zeros[:, 0:P], rhs=zeros[:], start=True, stop=True)
 
         x1_sb = keep.tile([P, SLOTS * D_IN], BF16, name="x1_sb")
         x1_rows = x1.rearrange("(g p t) d -> g p (t d)", p=P, t=PACK)

@@ -203,8 +203,10 @@ def tile_gcn_pb_kernel(tc, x1, adj, W1, b1, out):
                 transpose_x1(g + 2)
             if g > 0:
                 quantise_h(g - 1)
+        idle_ps = psum_mm.tile([P, D_OUT], F32, tag="mm")
         for a, b in halves:
             transpose_half(a, b)
+            nc.tensor.matmul(out=idle_ps[:], lhsT=ones[:], rhs=w1_sb[:], start=True, stop=True)
         quantise_h(PASSES - 1)
 
         for r in range(ROUNDS):

from contextlib import ExitStack

import concourse.mybir as mybir
from concourse.masks import make_identity

F32 = mybir.dt.float32
BF16 = mybir.dt.bfloat16
U32 = mybir.dt.uint32
U8 = mybir.dt.uint8
FP8X4 = mybir.dt.float8_e4m3fn_x4

P = 128
PACK = 4
K_PASS = P * PACK
BANK = 512

N_DST, N_SRC, D_IN, D_OUT = 2048, 2048, 128, 256
PASSES = N_SRC // K_PASS
DST_TILES = N_DST // P
SLOTS = PASSES * PACK
WORDS = N_SRC // 2
ROUND = 2
ROUNDS = DST_TILES // ROUND
LEAD = 5
STEPPED = LEAD

FLOPS = 2 * N_DST * N_SRC * D_OUT + 2 * N_SRC * D_IN * D_OUT


def tile_gcn_pb_kernel(tc, x1, adj, W1, b1, out):
    nc = tc.nc
    with ExitStack() as ctx:
        ctx.enter_context(tc.manual_schedule())
        keep = ctx.enter_context(tc.tile_pool(name="keep", bufs=1))
        stage = ctx.enter_context(tc.tile_pool(name="stage", bufs=8))
        psum_t = ctx.enter_context(tc.psum_pool(name="psum_t", bufs=6))
        psum_mm = ctx.enter_context(tc.psum_pool(name="psum_mm", bufs=2))

        bias_rows = keep.tile([P, D_OUT], BF16, name="bias_rows")
        nc.vector.memset(bias_rows[:], 0.0)

        x1_sb = keep.tile([P, SLOTS * D_IN], BF16, name="x1_sb")
        x1_rows = x1.rearrange("(g p t) d -> g p (t d)", p=P, t=PACK)
        w1_sb = keep.tile([P, D_OUT], BF16, name="w1_sb")
        nc.sync.dma_start(out=x1_sb[:, 0 : PACK * D_IN], in_=x1_rows[0])
        nc.sync.dma_start(out=w1_sb[:], in_=W1)
        nc.sync.dma_start(out=bias_rows[0:1, :], in_=b1.rearrange("(o f) -> o f", o=1))
        for g in range(1, PASSES):
            nc.sync.dma_start(
                out=x1_sb[:, g * PACK * D_IN : (g + 1) * PACK * D_IN], in_=x1_rows[g]
            )
        adj_rows = adj.rearrange("(p a) k -> p a k", a=DST_TILES)
        adj_sb = []
        for a in range(DST_TILES):
            adj_a = keep.tile([P, N_SRC], BF16, name="adj%d" % a)
            nc.sync.dma_start(out=adj_a[:], in_=adj_rows[:, a, :])
            adj_sb.append(adj_a)

        ident_bf = keep.tile([P, P], BF16, name="ident_bf")
        make_identity(nc, ident_bf[:])
        ones = keep.tile([P, P], BF16, name="ones")
        nc.vector.memset(ones[:], 1.0)
        ident_f32 = keep.tile([P, P], F32, name="ident_f32")
        make_identity(nc, ident_f32[:])
        bias_all = keep.tile([P, D_OUT], F32, name="bias_all")
        x1T = keep.tile([P, SLOTS * P], BF16, name="x1T")
        h_grouped = keep.tile([P, PASSES * D_OUT * PACK], BF16, name="h_grouped", align_bytes=64)
        h_grouped_v = h_grouped[:].rearrange("p (g f t) -> p g f t", g=PASSES, t=PACK)
        h_packed = keep.tile([P, PASSES * D_OUT], U32, name="h_packed", align_bytes=64)
        h_scales = keep.tile([P, PASSES * D_OUT], U8, name="h_scales", align_bytes=64)

        def spread_bias():
            bias_ps = psum_mm.tile([P, D_OUT], F32, tag="mm")
            nc.tensor.matmul(out=bias_ps[:], lhsT=ones[:], rhs=bias_rows[:], start=True, stop=True)
            nc.vector.tensor_copy(out=bias_all[:], in_=bias_ps[:])

        def transpose_x1(g):
            x1T_ps = psum_t.tile([P, PACK * P], BF16, tag="t")
            for t in range(PACK):
                s = PACK * g + t
                nc.tensor.transpose(
                    x1T_ps[:, t * P : (t + 1) * P], x1_sb[:, s * D_IN : (s + 1) * D_IN], ident_bf[:]
                )
            nc.scalar.copy(out=x1T[:, g * PACK * P : (g + 1) * PACK * P], in_=x1T_ps[:])

        def h_half(g, f0):
            h_ps = psum_mm.tile([P, BANK], F32, tag="mm")
            for t in range(PACK):
                s = PACK * g + t
                nc.tensor.matmul(
                    out=h_ps[:, t * P : (t + 1) * P],
                    lhsT=x1T[:, s * P : (s + 1) * P],
                    rhs=w1_sb[:, f0 : f0 + P],
                    start=True,
                    stop=True,
                )
            nc.vector.tensor_tensor(
                out=h_grouped_v[:, g, f0 : f0 + P, :],
                in0=h_ps[:].rearrange("p (t f) -> p f t", t=PACK),
                in1=bias_all[:, f0 : f0 + P].unsqueeze(2).to_broadcast([P, P, PACK]),
                op=mybir.AluOpType.add,
            )

        def quantise_h(g):
            words = slice(g * D_OUT, (g + 1) * D_OUT)
            nc.vector.quantize_mx(
                out=h_packed[:, words].bitcast(FP8X4),
                scales=h_scales[:, words],
                in_=h_grouped[:, g * D_OUT * PACK : (g + 1) * D_OUT * PACK],
            )

        even_odd = {}
        grouped = {}
        codes = {}

        def words_of(a):
            return adj_sb[a][:].bitcast(F32)

        def sort_tile(a):
            even_odd[a] = stage.tile([P, WORDS], F32, name="even_odd")
            nc.vector.tensor_copy(
                out=even_odd[a][:].rearrange("p (u w) -> p u w", u=2),
                in_=words_of(a).rearrange("p (w u) -> p u w", u=2),
            )

        def half_pass(a, g, u):
            if a < STEPPED:
                return words_of(a)[:, 2 * P * g + u : 2 * P * (g + 1) - 1 + u : 2]
            w0 = u * (WORDS // 2) + g * P
            return even_odd[a][:, w0 : w0 + P]

        def transpose_half(a, b):
            if b == 0:
                grouped[a] = stage.tile([P, N_SRC], BF16, name="grouped", align_bytes=64)
            adjT_ps = psum_t.tile([P, BANK], F32, tag="t")
            for j in range(BANK // P):
                nc.tensor.transpose(
                    adjT_ps[:, j * P : (j + 1) * P], half_pass(a, 2 * b + j // 2, j % 2), ident_f32[:]
                )
            nc.scalar.copy(
                out=grouped[a][:].bitcast(F32)[:, b * BANK : (b + 1) * BANK].rearrange(
                    "p (g i u) -> p g i u", i=P, u=2
                ),
                in_=adjT_ps[:].rearrange("p (g u i) -> p g i u", i=P, u=2),
            )

        def transpose_tile(a):
            for b in range(WORDS // BANK):
                transpose_half(a, b)

        def quantise_tile(a):
            packed = stage.tile([P, PASSES * P], U32, name="adj_packed", align_bytes=64)
            scales = stage.tile([P, PASSES * P], U8, name="adj_scales", align_bytes=64)
            nc.vector.quantize_mx(out=packed[:].bitcast(FP8X4), scales=scales[:], in_=grouped[a][:])
            codes[a] = (packed, scales)

        def multiply_tile(a, acc):
            packed, scales = codes[a]
            for g in range(PASSES):
                nc.tensor.matmul_mx(
                    out=acc,
                    lhsT=packed[:, g * P : (g + 1) * P].bitcast(FP8X4),
                    lhsT_scale=scales[:, g * P : (g + 1) * P],
                    rhs=h_packed[:, g * D_OUT : (g + 1) * D_OUT].bitcast(FP8X4),
                    rhs_scale=h_scales[:, g * D_OUT : (g + 1) * D_OUT],
                    start=(g == 0),
                    stop=(g == PASSES - 1),
                )

        def tiles_of(r):
            return range(r * ROUND, (r + 1) * ROUND) if r < ROUNDS else range(0)

        out_sb = keep.tile([P, DST_TILES * D_OUT], F32, name="out_sb")
        out_rows = out.rearrange("(p a) f -> p (a f)", a=DST_TILES)

        def finish_round(r):
            acc = psum_mm.tile([P, BANK], F32, tag="mm")
            for a in tiles_of(r):
                multiply_tile(a, acc[:, (a % ROUND) * D_OUT : (a % ROUND + 1) * D_OUT])
            cols = slice(r * BANK, (r + 1) * BANK)
            nc.scalar.activation(
                out=out_sb[:, cols], in_=acc[:], func=mybir.ActivationFunctionType.Relu
            )
            nc.sync.dma_start(out=out_rows[:, cols], in_=out_sb[:, cols])

        def finish_tile(a):
            acc = psum_t.tile([P, D_OUT], F32, tag="t")
            multiply_tile(a, acc[:])
            cols = slice(a * D_OUT, (a + 1) * D_OUT)
            nc.vector.tensor_scalar_max(out=out_sb[:, cols], in0=acc[:], scalar1=0.0)
            nc.sync.dma_start(out=out_rows[:, cols], in_=out_sb[:, cols])

        transpose_x1(0)
        spread_bias()
        transpose_x1(1)
        halves = [(a, b) for a in range(LEAD) for b in range(WORDS // BANK)]
        for g in range(PASSES):
            for f0 in range(0, D_OUT, P):
                if g > 0:
                    transpose_half(*halves.pop(0))
                h_half(g, f0)
            if g + 2 < PASSES:
                transpose_x1(g + 2)
            if g > 0:
                quantise_h(g - 1)
        idle_ps = psum_mm.tile([P, D_OUT], F32, tag="mm")
        for a, b in halves:
            transpose_half(a, b)
            nc.tensor.matmul(out=idle_ps[:], lhsT=ones[:], rhs=w1_sb[:], start=True, stop=True)
        quantise_h(PASSES - 1)

        for r in range(ROUNDS):
            for a in tiles_of(r):
                if a + LEAD < DST_TILES:
                    sort_tile(a + LEAD)
                quantise_tile(a)
            for a in tiles_of(r):
                if a + LEAD < DST_TILES:
                    transpose_tile(a + LEAD)
            if r < ROUNDS - 1:
                finish_round(r)
            else:
                for a in tiles_of(r):
                    finish_tile(a)
